import numpy as np
import ml_dtypes


def mxq(x, axis, fmt="e4m3"):
    dtype, down = {"e4m3": (ml_dtypes.float8_e4m3fn, 7), "e5m2": (ml_dtypes.float8_e5m2, 14)}[fmt]
    v = np.moveaxis(np.asarray(x, np.float32).astype(ml_dtypes.bfloat16).astype(np.float64), axis, -1)
    blocks = v.reshape(v.shape[:-1] + (-1, 32))
    amax = np.abs(blocks).max(-1, keepdims=True)
    byte = np.maximum(np.where(amax > 0, np.frexp(amax)[1] - 1 + 127, 0) - down, 1)
    scale = np.exp2(byte - 127.0)
    codes = (blocks / scale).astype(np.float32).astype(dtype).astype(np.float64)
    return np.moveaxis((codes * scale).reshape(v.shape), -1, axis)


WIDE = False


def mx_kscale(k):
    if not WIDE:
        return np.ones(k)
    levels = np.array([20, -20, 10, -10, 0])
    a = np.random.permutation(np.resize(levels, k // 512 * 4)).reshape(k // 512, 4)
    idx = np.arange(k)
    return np.exp2(a[idx // 512, idx % 128 // 32])


BF16 = ml_dtypes.bfloat16


def bf(x):
    return np.asarray(x, np.float32).astype(BF16)


def f64(x):
    return np.asarray(x).astype(np.float64)


B, N, C, H, F = 2, 512, 1024, 8, 2752
D = C // H


def setup_inputs():
    u = mx_kscale(C)
    z = np.random.standard_normal((B, H, D, D)) * np.sqrt((N + N * N / C) / D)
    e = np.exp(z - z.max(-1, keepdims=True))
    attn = e / e.sum(-1, keepdims=True)
    v = np.random.standard_normal((B, H, N, D))
    w_proj = np.random.standard_normal((C, C)) / np.sqrt(C) / u[:, None]
    b_proj = 0.1 * np.random.standard_normal(C)
    shortcut = np.random.standard_normal((B, N, C))
    g = np.random.standard_normal((B, N, C)) * np.exp2(np.random.randint(-12, 1, (B, N, 1))) * 16.0 * u
    return {"attn": bf(attn), "v": bf(v), "w_proj": bf(w_proj), "b_proj": bf(b_proj),
            "shortcut": bf(shortcut), "grad_out": bf(g)}


def reference(attn, v, w_proj, b_proj, shortcut, grad_out):
    dy = mxq(f64(grad_out), 2, "e5m2") @ mxq(f64(w_proj), 0, "e4m3")
    do = dy.reshape(B, H, N, D)
    return do @ f64(attn)

@@ -1,0 +1,203 @@
+import concourse.mybir as mybir
+from concourse.masks import make_identity
+
+BF16 = mybir.dt.bfloat16
+F32 = mybir.dt.float32
+U32 = mybir.dt.uint32
+U8 = mybir.dt.uint8
+E4M3_X4 = mybir.dt.float8_e4m3fn_x4
+E5M2_X4 = mybir.dt.float8_e5m2_x4
+
+P = 128
+BATCH = 2
+TOKENS = 512
+FEAT = 1024
+HEADS = 8
+HEAD_DIM = 128
+PACK = 4
+K_PASS = P * PACK
+PASSES = FEAT // K_PASS
+WORD_BLOCKS = 2
+TOKEN_TILES = TOKENS // P
+HEAD_ROWS = TOKENS // HEADS
+PAIR = 2
+ROUNDS = FEAT // (PAIR * HEAD_DIM)
+QUARTER = PAIR * HEAD_DIM
+HALF_HEADS = HEADS // 2
+HALF_TOKENS = TOKENS // 2
+
+FLOPS = 2 * BATCH * TOKENS * FEAT * FEAT + 2 * BATCH * HEADS * TOKENS * HEAD_DIM * HEAD_DIM
+BYTES = 2 * (BATCH * TOKENS * FEAT + FEAT * FEAT + BATCH * HEADS * HEAD_DIM * HEAD_DIM) + 4 * BATCH * TOKENS * FEAT
+
+
+def tile_transposedattentiontransformer_pb_kernel(
+    tc, attn, v, w_proj, b_proj, shortcut, grad_out, out
+):
+    nc = tc.nc
+    grad_rows = grad_out.flatten_outer_dims()
+    out_view = out.rearrange(
+        "b g (rr pair half) e -> b pair half rr g e", pair=ROUNDS, half=PAIR
+    )
+
+    with tc.tile_pool(name="keep", bufs=1) as keep, tc.tile_pool(
+        name="work", bufs=3
+    ) as work, tc.psum_pool(name="psum_t", bufs=2) as psum_t, tc.psum_pool(
+        name="psum_dy", bufs=4
+    ) as psum_dy, tc.psum_pool(name="psum_o", bufs=2) as psum_o:
+        grad_raw = keep.tile([P, BATCH * TOKEN_TILES, FEAT], BF16)
+        grad_grouped = keep.tile([P, BATCH, PASSES, TOKENS, PACK], BF16, align_bytes=64)
+        grad_codes = keep.tile([P, BATCH, PASSES, TOKENS], U32, align_bytes=64)
+        grad_scales = keep.tile([P, BATCH, PASSES, TOKENS], U8, align_bytes=64)
+        w_raw = keep.tile([P, ROUNDS, PASSES, PACK, QUARTER], BF16)
+        w_grouped = keep.tile([P, ROUNDS, PASSES, QUARTER, PACK], BF16, align_bytes=64)
+        w_codes = keep.tile([P, ROUNDS, PASSES, QUARTER], U32, align_bytes=64)
+        w_scales = keep.tile([P, ROUNDS, PASSES, QUARTER], U8, align_bytes=64)
+        attn_raw = keep.tile([P, BATCH * HEADS, HEAD_DIM], BF16)
+        attn_f32 = keep.tile([P, BATCH * HEADS, HEAD_DIM], F32)
+        identity = keep.tile([P, P], F32)
+
+        grad_words = grad_raw[:].bitcast(F32)
+        grouped_words = grad_grouped[:].bitcast(F32)
+
+        def load_w(pair):
+            cols = slice(pair * QUARTER, (pair + 1) * QUARTER)
+            for s in range(PASSES):
+                for u in range(WORD_BLOCKS):
+                    first = s * K_PASS + u * 2 * P
+                    nc.sync.dma_start(
+                        out=w_raw[:, pair, s, 2 * u : 2 * u + 2, :],
+                        in_=w_proj[first : first + 2 * P, cols].rearrange(
+                            "(p e) c -> p e c", e=2
+                        ),
+                    )
+
+        def load_grad(tile_index):
+            rows = slice(tile_index * P, (tile_index + 1) * P)
+            nc.sync.dma_start(out=grad_raw[:, tile_index, :], in_=grad_rows[rows, :])
+
+        def load_attn(b):
+            heads = slice(b * HEADS, (b + 1) * HEADS)
+            nc.sync.dma_start(
+                out=attn_raw[:, heads, :], in_=attn[b].rearrange("g d e -> d g e")
+            )
+
+        def quantise_w(pair):
+            for s in range(PASSES):
+                nc.vector.tensor_copy(
+                    out=w_grouped[:, pair, s, :, :].rearrange("p (c i) t -> p c t i", i=4),
+                    in_=w_raw[:, pair, s, :, :].rearrange("p t (c i) -> p c t i", i=4),
+                )
+            for s in range(PASSES):
+                nc.vector.quantize_mx(
+                    out=w_codes[:, pair, s, :].bitcast(E4M3_X4),
+                    scales=w_scales[:, pair, s, :],
+                    in_=w_grouped[:, pair, s, :, :].rearrange("p c t -> p (c t)"),
+                )
+
+        def transpose_grad(tile_index):
+            b, tile_in_batch = divmod(tile_index, TOKEN_TILES)
+            flipped = psum_t.tile([P, PASSES * WORD_BLOCKS, P], F32)
+            for block in range(PASSES * WORD_BLOCKS):
+                nc.tensor.transpose(
+                    flipped[:, block, :],
+                    grad_words[:, tile_index, block * P : (block + 1) * P],
+                    identity[:],
+                )
+            tokens = slice(tile_in_batch * P, (tile_in_batch + 1) * P)
+            nc.scalar.copy(
+                out=grouped_words[:, b, :, tokens, :],
+                in_=flipped[:].rearrange("p (s u) tok -> p s tok u", u=WORD_BLOCKS),
+            )
+
+        def quantise_grad(b, half):
+            tokens = slice(half * HALF_TOKENS, (half + 1) * HALF_TOKENS)
+            for s in range(PASSES):
+                nc.vector.quantize_mx(
+                    out=grad_codes[:, b, s, tokens].bitcast(E5M2_X4),
+                    scales=grad_scales[:, b, s, tokens],
+                    in_=grad_grouped[:, b, s, tokens, :].rearrange("p tok t -> p (tok t)"),
+                )
+
+        def widen_attn(b):
+            heads = slice(b * HEADS, (b + 1) * HEADS)
+            nc.scalar.copy(out=attn_f32[:, heads, :], in_=attn_raw[:, heads, :])
+
+        def project(b, pair):
+            dy_t = work.tile([P, HEADS, PAIR, HEAD_ROWS], F32, tag="dy_t")
+            for half in range(PAIR):
+                cols = slice(half * HEAD_DIM, (half + 1) * HEAD_DIM)
+                acc = psum_dy.tile([P, TOKENS], F32)
+                for s in range(PASSES):
+                    nc.tensor.matmul_mx(
+                        out=acc[:],
+                        lhsT=w_codes[:, pair, s, cols].bitcast(E4M3_X4),
+                        lhsT_scale=w_scales[:, pair, s, cols],
+                        rhs=grad_codes[:, b, s, :].bitcast(E5M2_X4),
+                        rhs_scale=grad_scales[:, b, s, :],
+                        start=(s == 0),
+                        stop=(s == PASSES - 1),
+                    )
+                by_head = acc[:].rearrange("p (g rr) -> p g rr", rr=HEAD_ROWS)
+                if half == 0:
+                    nc.scalar.copy(out=dy_t[:, :, half, :], in_=by_head)
+                else:
+                    nc.vector.tensor_copy(out=dy_t[:, :, half, :], in_=by_head)
+            return dy_t
+
+        def apply_attn(b, pair, dy_t):
+            result = work.tile([P, HEADS, HEAD_DIM], F32, tag="result")
+            for group in range(HEADS // HALF_HEADS):
+                product = psum_o.tile([P, HALF_HEADS, HEAD_DIM], F32)
+                for i in range(HALF_HEADS):
+                    g = group * HALF_HEADS + i
+                    nc.tensor.matmul(
+                        out=product[:, i, :],
+                        lhsT=dy_t[:, g, :, :].rearrange("p half rr -> p (half rr)"),
+                        rhs=attn_f32[:, b * HEADS + g, :],
+                        start=True,
+                        stop=True,
+                    )
+                heads = slice(group * HALF_HEADS, (group + 1) * HALF_HEADS)
+                if group == 0:
+                    nc.scalar.copy(out=result[:, heads, :], in_=product[:])
+                else:
+                    nc.vector.tensor_copy(out=result[:, heads, :], in_=product[:])
+                for half in range(PAIR):
+                    rows = slice(half * HEAD_ROWS, (half + 1) * HEAD_ROWS)
+                    nc.sync.dma_start(
+                        out=out_view[b, pair, half, :, heads, :], in_=result[rows, heads, :]
+                    )
+
+        load_w(0)
+        for tile_index in range(TOKEN_TILES):
+            load_grad(tile_index)
+        load_attn(0)
+        for pair in range(1, ROUNDS):
+            load_w(pair)
+        for tile_index in range(TOKEN_TILES, BATCH * TOKEN_TILES):
+            load_grad(tile_index)
+        load_attn(1)
+        make_identity(nc, identity[:])
+
+        quantise_w(0)
+        for half in range(2):
+            transpose_grad(2 * half)
+            transpose_grad(2 * half + 1)
+            quantise_grad(0, half)
+        widen_attn(0)
+
+        rounds = [(b, pair) for b in range(BATCH) for pair in range(ROUNDS)]
+        dy_ready = project(0, 0)
+        for r, (b, pair) in enumerate(rounds):
+            dy_now = dy_ready
+            if r + 1 < ROUNDS:
+                quantise_w(r + 1)
+            if r + 1 < len(rounds):
+                dy_ready = project(rounds[r + 1][0], rounds[r + 1][1])
+            apply_attn(b, pair, dy_now)
+            if r in (1, 2):
+                transpose_grad(TOKEN_TILES + 2 * (r - 1))
+                transpose_grad(TOKEN_TILES + 2 * (r - 1) + 1)
+                quantise_grad(1, r - 1)
+            if r == 2:
+                widen_attn(1)

@@ -41,9 +41,9 @@ def tile_transposedattentiontransformer_pb_kernel(
 
     with tc.tile_pool(name="keep", bufs=1) as keep, tc.tile_pool(
         name="work", bufs=3
-    ) as work, tc.psum_pool(name="psum_t", bufs=2) as psum_t, tc.psum_pool(
-        name="psum_dy", bufs=4
-    ) as psum_dy, tc.psum_pool(name="psum_o", bufs=2) as psum_o:
+    ) as work, tc.psum_pool(name="psum_in", bufs=6) as psum_in, tc.psum_pool(
+        name="psum_o", bufs=2
+    ) as psum_o, tc.manual_schedule():
         grad_raw = keep.tile([P, BATCH * TOKEN_TILES, FEAT], BF16)
         grad_grouped = keep.tile([P, BATCH, PASSES, TOKENS, PACK], BF16, align_bytes=64)
         grad_codes = keep.tile([P, BATCH, PASSES, TOKENS], U32, align_bytes=64)
@@ -96,7 +96,7 @@ def tile_transposedattentiontransformer_pb_kernel(
 
         def transpose_grad(tile_index):
             b, tile_in_batch = divmod(tile_index, TOKEN_TILES)
-            flipped = psum_t.tile([P, PASSES * WORD_BLOCKS, P], F32)
+            flipped = psum_in.tile([P, PASSES * WORD_BLOCKS, P], F32, tag="bank")
             for block in range(PASSES * WORD_BLOCKS):
                 nc.tensor.transpose(
                     flipped[:, block, :],
@@ -120,13 +120,13 @@ def tile_transposedattentiontransformer_pb_kernel(
 
         def widen_attn(b):
             heads = slice(b * HEADS, (b + 1) * HEADS)
-            nc.scalar.copy(out=attn_f32[:, heads, :], in_=attn_raw[:, heads, :])
+            nc.vector.tensor_copy(out=attn_f32[:, heads, :], in_=attn_raw[:, heads, :])
 
         def project(b, pair):
             dy_t = work.tile([P, HEADS, PAIR, HEAD_ROWS], F32, tag="dy_t")
             for half in range(PAIR):
                 cols = slice(half * HEAD_DIM, (half + 1) * HEAD_DIM)
-                acc = psum_dy.tile([P, TOKENS], F32)
+                acc = psum_in.tile([P, TOKENS], F32, tag="bank")
                 for s in range(PASSES):
                     nc.tensor.matmul_mx(
                         out=acc[:],
@@ -138,10 +138,7 @@ def tile_transposedattentiontransformer_pb_kernel(
                         stop=(s == PASSES - 1),
                     )
                 by_head = acc[:].rearrange("p (g rr) -> p g rr", rr=HEAD_ROWS)
-                if half == 0:
-                    nc.scalar.copy(out=dy_t[:, :, half, :], in_=by_head)
-                else:
-                    nc.vector.tensor_copy(out=dy_t[:, :, half, :], in_=by_head)
+                nc.scalar.copy(out=dy_t[:, :, half, :], in_=by_head)
             return dy_t
 
         def apply_attn(b, pair, dy_t):
@@ -180,24 +177,28 @@ def tile_transposedattentiontransformer_pb_kernel(
         make_identity(nc, identity[:])
 
         quantise_w(0)
+        for tile_index in range(TOKEN_TILES):
+            transpose_grad(tile_index)
         for half in range(2):
-            transpose_grad(2 * half)
-            transpose_grad(2 * half + 1)
             quantise_grad(0, half)
         widen_attn(0)
+        quantise_w(1)
 
         rounds = [(b, pair) for b in range(BATCH) for pair in range(ROUNDS)]
-        dy_ready = project(0, 0)
-        for r, (b, pair) in enumerate(rounds):
-            dy_now = dy_ready
-            if r + 1 < ROUNDS:
-                quantise_w(r + 1)
-            if r + 1 < len(rounds):
-                dy_ready = project(rounds[r + 1][0], rounds[r + 1][1])
-            apply_attn(b, pair, dy_now)
-            if r in (1, 2):
-                transpose_grad(TOKEN_TILES + 2 * (r - 1))
-                transpose_grad(TOKEN_TILES + 2 * (r - 1) + 1)
-                quantise_grad(1, r - 1)
-            if r == 2:
+        dy_now = project(0, 0)
+        quantise_w(2)
+        apply_attn(0, 0, dy_now)
+        dy_now = project(0, 1)
+        for r in range(1, len(rounds)):
+            if r + 2 < ROUNDS:
+                quantise_w(r + 2)
+            if r == ROUNDS - 2:
+                for tile_index in range(TOKEN_TILES, BATCH * TOKEN_TILES):
+                    transpose_grad(tile_index)
+                for half in range(2):
+                    quantise_grad(1, half)
                 widen_attn(1)
+            if r + 1 < len(rounds):
+                dy_next = project(rounds[r + 1][0], rounds[r + 1][1])
+            apply_attn(rounds[r][0], rounds[r][1], dy_now)
+            dy_now = dy_next

@@ -19,6 +19,7 @@ K_PASS = P * PACK
 PASSES = FEAT // K_PASS
 WORD_BLOCKS = 2
 TOKEN_TILES = TOKENS // P
+HALF_TILES = TOKEN_TILES // 2
 HEAD_ROWS = TOKENS // HEADS
 PAIR = 2
 ROUNDS = FEAT // (PAIR * HEAD_DIM)
@@ -34,7 +35,6 @@ def tile_transposedattentiontransformer_pb_kernel(
     tc, attn, v, w_proj, b_proj, shortcut, grad_out, out
 ):
     nc = tc.nc
-    grad_rows = grad_out.flatten_outer_dims()
     out_view = out.rearrange(
         "b g (rr pair half) e -> b pair half rr g e", pair=ROUNDS, half=PAIR
     )
@@ -44,7 +44,7 @@ def tile_transposedattentiontransformer_pb_kernel(
     ) as work, tc.psum_pool(name="psum_in", bufs=6) as psum_in, tc.psum_pool(
         name="psum_o", bufs=2
     ) as psum_o, tc.manual_schedule():
-        grad_raw = keep.tile([P, BATCH * TOKEN_TILES, FEAT], BF16)
+        grad_raw = keep.tile([P, BATCH, TOKEN_TILES, FEAT], BF16)
         grad_grouped = keep.tile([P, BATCH, PASSES, TOKENS, PACK], BF16, align_bytes=64)
         grad_codes = keep.tile([P, BATCH, PASSES, TOKENS], U32, align_bytes=64)
         grad_scales = keep.tile([P, BATCH, PASSES, TOKENS], U8, align_bytes=64)
@@ -52,84 +52,93 @@ def tile_transposedattentiontransformer_pb_kernel(
         w_grouped = keep.tile([P, ROUNDS, PASSES, QUARTER, PACK], BF16, align_bytes=64)
         w_codes = keep.tile([P, ROUNDS, PASSES, QUARTER], U32, align_bytes=64)
         w_scales = keep.tile([P, ROUNDS, PASSES, QUARTER], U8, align_bytes=64)
-        attn_raw = keep.tile([P, BATCH * HEADS, HEAD_DIM], BF16)
-        attn_f32 = keep.tile([P, BATCH * HEADS, HEAD_DIM], F32)
+        attn_raw = keep.tile([P, BATCH, HEADS, HEAD_DIM], BF16)
+        attn_f32 = keep.tile([P, BATCH, HEADS, HEAD_DIM], F32)
         identity = keep.tile([P, P], F32)
 
         grad_words = grad_raw[:].bitcast(F32)
         grouped_words = grad_grouped[:].bitcast(F32)
 
-        def load_w(pair):
+        def load_w(pair, s):
             cols = slice(pair * QUARTER, (pair + 1) * QUARTER)
-            for s in range(PASSES):
-                for u in range(WORD_BLOCKS):
-                    first = s * K_PASS + u * 2 * P
-                    nc.sync.dma_start(
-                        out=w_raw[:, pair, s, 2 * u : 2 * u + 2, :],
-                        in_=w_proj[first : first + 2 * P, cols].rearrange(
-                            "(p e) c -> p e c", e=2
-                        ),
-                    )
+            for u in range(WORD_BLOCKS):
+                first = s * K_PASS + u * 2 * P
+                nc.sync.dma_start(
+                    out=w_raw[:, pair, s, 2 * u : 2 * u + 2, :],
+                    in_=w_proj[first : first + 2 * P, cols].rearrange("(p e) c -> p e c", e=2),
+                )
 
-        def load_grad(tile_index):
-            rows = slice(tile_index * P, (tile_index + 1) * P)
-            nc.sync.dma_start(out=grad_raw[:, tile_index, :], in_=grad_rows[rows, :])
+        def load_grad(b, s, token_half):
+            tiles = slice(token_half * HALF_TILES, (token_half + 1) * HALF_TILES)
+            tokens = slice(token_half * HALF_TOKENS, (token_half + 1) * HALF_TOKENS)
+            js = slice(s * K_PASS, (s + 1) * K_PASS)
+            nc.sync.dma_start(
+                out=grad_raw[:, b, tiles, js],
+                in_=grad_out[b, tokens, js].rearrange("(i p) j -> p i j", p=P),
+            )
 
         def load_attn(b):
-            heads = slice(b * HEADS, (b + 1) * HEADS)
-            nc.sync.dma_start(
-                out=attn_raw[:, heads, :], in_=attn[b].rearrange("g d e -> d g e")
+            nc.sync.dma_start(out=attn_raw[:, b, :, :], in_=attn[b].rearrange("g d e -> d g e"))
+
+        def regroup_w(pair, s):
+            nc.vector.tensor_copy(
+                out=w_grouped[:, pair, s, :, :].rearrange("p (c i) t -> p c t i", i=4),
+                in_=w_raw[:, pair, s, :, :].rearrange("p t (c i) -> p c t i", i=4),
             )
 
-        def quantise_w(pair):
-            for s in range(PASSES):
-                nc.vector.tensor_copy(
-                    out=w_grouped[:, pair, s, :, :].rearrange("p (c i) t -> p c t i", i=4),
-                    in_=w_raw[:, pair, s, :, :].rearrange("p t (c i) -> p c t i", i=4),
-                )
-            for s in range(PASSES):
-                nc.vector.quantize_mx(
-                    out=w_codes[:, pair, s, :].bitcast(E4M3_X4),
-                    scales=w_scales[:, pair, s, :],
-                    in_=w_grouped[:, pair, s, :, :].rearrange("p c t -> p (c t)"),
-                )
+        def quantise_w(pair, s):
+            nc.vector.quantize_mx(
+                out=w_codes[:, pair, s, :].bitcast(E4M3_X4),
+                scales=w_scales[:, pair, s, :],
+                in_=w_grouped[:, pair, s, :, :].rearrange("p c t -> p (c t)"),
+            )
 
-        def transpose_grad(tile_index):
-            b, tile_in_batch = divmod(tile_index, TOKEN_TILES)
-            flipped = psum_in.tile([P, PASSES * WORD_BLOCKS, P], F32, tag="bank")
-            for block in range(PASSES * WORD_BLOCKS):
-                nc.tensor.transpose(
-                    flipped[:, block, :],
-                    grad_words[:, tile_index, block * P : (block + 1) * P],
-                    identity[:],
-                )
-            tokens = slice(tile_in_batch * P, (tile_in_batch + 1) * P)
+        def prepare_w(pair):
+            for s in range(PASSES):
+                regroup_w(pair, s)
+            for s in range(PASSES):
+                quantise_w(pair, s)
+
+        def transpose_grad(b, s, token_half):
+            flipped = psum_in.tile([P, HALF_TILES, WORD_BLOCKS, P], F32, tag="bank")
+            for i in range(HALF_TILES):
+                for u in range(WORD_BLOCKS):
+                    first = (s * WORD_BLOCKS + u) * P
+                    nc.tensor.transpose(
+                        flipped[:, i, u, :],
+                        grad_words[:, b, token_half * HALF_TILES + i, first : first + P],
+                        identity[:],
+                    )
+            tokens = slice(token_half * HALF_TOKENS, (token_half + 1) * HALF_TOKENS)
             nc.scalar.copy(
-                out=grouped_words[:, b, :, tokens, :],
-                in_=flipped[:].rearrange("p (s u) tok -> p s tok u", u=WORD_BLOCKS),
+                out=grouped_words[:, b, s, tokens, :].rearrange("p (i tok) u -> p i tok u", tok=P),
+                in_=flipped[:].rearrange("p i u tok -> p i tok u"),
             )
 
-        def quantise_grad(b, half):
-            tokens = slice(half * HALF_TOKENS, (half + 1) * HALF_TOKENS)
-            for s in range(PASSES):
-                nc.vector.quantize_mx(
-                    out=grad_codes[:, b, s, tokens].bitcast(E5M2_X4),
-                    scales=grad_scales[:, b, s, tokens],
-                    in_=grad_grouped[:, b, s, tokens, :].rearrange("p tok t -> p (tok t)"),
-                )
+        def quantise_grad(b, s, token_half):
+            tokens = slice(token_half * HALF_TOKENS, (token_half + 1) * HALF_TOKENS)
+            nc.vector.quantize_mx(
+                out=grad_codes[:, b, s, tokens].bitcast(E5M2_X4),
+                scales=grad_scales[:, b, s, tokens],
+                in_=grad_grouped[:, b, s, tokens, :].rearrange("p tok t -> p (tok t)"),
+            )
 
-        def widen_attn(b):
-            heads = slice(b * HEADS, (b + 1) * HEADS)
-            nc.vector.tensor_copy(out=attn_f32[:, heads, :], in_=attn_raw[:, heads, :])
+        def prepare_grad(b, s):
+            for token_half in range(2):
+                transpose_grad(b, s, token_half)
+            for token_half in range(2):
+                quantise_grad(b, s, token_half)
 
         def project(b, pair):
-            dy_t = work.tile([P, HEADS, PAIR, HEAD_ROWS], F32, tag="dy_t")
+            banks = []
             for half in range(PAIR):
-                cols = slice(half * HEAD_DIM, (half + 1) * HEAD_DIM)
-                acc = psum_in.tile([P, TOKENS], F32, tag="bank")
-                for s in range(PASSES):
+                acc = psum_in.tile([P, HEADS, HEAD_ROWS], F32, tag="bank")
+                banks.append(acc)
+            for s in range(PASSES):
+                for half in range(PAIR):
+                    cols = slice(half * HEAD_DIM, (half + 1) * HEAD_DIM)
                     nc.tensor.matmul_mx(
-                        out=acc[:],
+                        out=banks[half][:].rearrange("p g rr -> p (g rr)"),
                         lhsT=w_codes[:, pair, s, cols].bitcast(E4M3_X4),
                         lhsT_scale=w_scales[:, pair, s, cols],
                         rhs=grad_codes[:, b, s, :].bitcast(E5M2_X4),
@@ -137,8 +146,11 @@ def tile_transposedattentiontransformer_pb_kernel(
                         start=(s == 0),
                         stop=(s == PASSES - 1),
                     )
-                by_head = acc[:].rearrange("p (g rr) -> p g rr", rr=HEAD_ROWS)
-                nc.scalar.copy(out=dy_t[:, :, half, :], in_=by_head)
+            dy_t = work.tile([P, HEADS, PAIR, HEAD_ROWS], F32, tag="dy_t")
+            for group in range(HEADS // HALF_HEADS):
+                heads = slice(group * HALF_HEADS, (group + 1) * HALF_HEADS)
+                for half in range(PAIR):
+                    nc.scalar.copy(out=dy_t[:, heads, half, :], in_=banks[half][:, heads, :])
             return dy_t
 
         def apply_attn(b, pair, dy_t):
@@ -150,7 +162,7 @@ def tile_transposedattentiontransformer_pb_kernel(
                     nc.tensor.matmul(
                         out=product[:, i, :],
                         lhsT=dy_t[:, g, :, :].rearrange("p half rr -> p (half rr)"),
-                        rhs=attn_f32[:, b * HEADS + g, :],
+                        rhs=attn_f32[:, b, g, :],
                         start=True,
                         stop=True,
                     )
@@ -165,39 +177,39 @@ def tile_transposedattentiontransformer_pb_kernel(
                         out=out_view[b, pair, half, :, heads, :], in_=result[rows, heads, :]
                     )
 
-        load_w(0)
-        for tile_index in range(TOKEN_TILES):
-            load_grad(tile_index)
+        for s in range(PASSES):
+            load_w(0, s)
+            for token_half in range(2):
+                load_grad(0, s, token_half)
         load_attn(0)
         for pair in range(1, ROUNDS):
-            load_w(pair)
-        for tile_index in range(TOKEN_TILES, BATCH * TOKEN_TILES):
-            load_grad(tile_index)
+            for s in range(PASSES):
+                load_w(pair, s)
+        for s in range(PASSES):
+            for token_half in range(2):
+                load_grad(1, s, token_half)
         load_attn(1)
         make_identity(nc, identity[:])
 
-        quantise_w(0)
-        for tile_index in range(TOKEN_TILES):
-            transpose_grad(tile_index)
-        for half in range(2):
-            quantise_grad(0, half)
-        widen_attn(0)
-        quantise_w(1)
+        for s in range(PASSES):
+            regroup_w(0, s)
+            quantise_w(0, s)
+            prepare_grad(0, s)
+        nc.scalar.copy(out=attn_f32[:, 0, :, :], in_=attn_raw[:, 0, :, :])
 
         rounds = [(b, pair) for b in range(BATCH) for pair in range(ROUNDS)]
         dy_now = project(0, 0)
-        quantise_w(2)
+        prepare_w(1)
+        prepare_w(2)
         apply_attn(0, 0, dy_now)
         dy_now = project(0, 1)
         for r in range(1, len(rounds)):
             if r + 2 < ROUNDS:
-                quantise_w(r + 2)
+                prepare_w(r + 2)
             if r == ROUNDS - 2:
-                for tile_index in range(TOKEN_TILES, BATCH * TOKEN_TILES):
-                    transpose_grad(tile_index)
-                for half in range(2):
-                    quantise_grad(1, half)
-                widen_attn(1)
+                for s in range(PASSES):
+                    prepare_grad(1, s)
+                nc.vector.tensor_copy(out=attn_f32[:, 1, :, :], in_=attn_raw[:, 1, :, :])
             if r + 1 < len(rounds):
                 dy_next = project(rounds[r + 1][0], rounds[r + 1][1])
             apply_attn(rounds[r][0], rounds[r][1], dy_now)

@@ -55,9 +55,17 @@ def tile_transposedattentiontransformer_pb_kernel(
         attn_raw = keep.tile([P, BATCH, HEADS, HEAD_DIM], BF16)
         attn_f32 = keep.tile([P, BATCH, HEADS, HEAD_DIM], F32)
         identity = keep.tile([P, P], F32)
+        idle_operand = keep.tile([P, P], F32)
 
         grad_words = grad_raw[:].bitcast(F32)
         grouped_words = grad_grouped[:].bitcast(F32)
+
+        def warm_up(count):
+            for i in range(count):
+                product = psum_o.tile([P, HALF_HEADS, HEAD_DIM], F32, tag="product")
+                nc.tensor.matmul(
+                    out=product[:, 0, :], lhsT=idle_operand[:], rhs=idle_operand[:], start=True, stop=True
+                )
 
         def load_w(pair, s):
             cols = slice(pair * QUARTER, (pair + 1) * QUARTER)
@@ -109,6 +117,8 @@ def tile_transposedattentiontransformer_pb_kernel(
                         grad_words[:, b, token_half * HALF_TILES + i, first : first + P],
                         identity[:],
                     )
+            if b == 0:
+                warm_up(1)
             tokens = slice(token_half * HALF_TOKENS, (token_half + 1) * HALF_TOKENS)
             nc.scalar.copy(
                 out=grouped_words[:, b, s, tokens, :].rearrange("p (i tok) u -> p i tok u", tok=P),
@@ -156,7 +166,7 @@ def tile_transposedattentiontransformer_pb_kernel(
         def apply_attn(b, pair, dy_t):
             result = work.tile([P, HEADS, HEAD_DIM], F32, tag="result")
             for group in range(HEADS // HALF_HEADS):
-                product = psum_o.tile([P, HALF_HEADS, HEAD_DIM], F32)
+                product = psum_o.tile([P, HALF_HEADS, HEAD_DIM], F32, tag="product")
                 for i in range(HALF_HEADS):
                     g = group * HALF_HEADS + i
                     nc.tensor.matmul(
@@ -190,6 +200,8 @@ def tile_transposedattentiontransformer_pb_kernel(
                 load_grad(1, s, token_half)
         load_attn(1)
         make_identity(nc, identity[:])
+        nc.vector.memset(idle_operand[:], 0.0)
+        warm_up(6)
 
         for s in range(PASSES):
             regroup_w(0, s)

@@ -44,7 +44,7 @@ def tile_transposedattentiontransformer_pb_kernel(
     ) as work, tc.psum_pool(name="psum_in", bufs=6) as psum_in, tc.psum_pool(
         name="psum_o", bufs=2
     ) as psum_o, tc.manual_schedule():
-        grad_raw = keep.tile([P, BATCH, TOKEN_TILES, FEAT], BF16)
+        grad_words = {}
         grad_grouped = keep.tile([P, BATCH, PASSES, TOKENS, PACK], BF16, align_bytes=64)
         grad_codes = keep.tile([P, BATCH, PASSES, TOKENS], U32, align_bytes=64)
         grad_scales = keep.tile([P, BATCH, PASSES, TOKENS], U8, align_bytes=64)
@@ -57,8 +57,13 @@ def tile_transposedattentiontransformer_pb_kernel(
         identity = keep.tile([P, P], F32)
         idle_operand = keep.tile([P, P], F32)
 
-        grad_words = grad_raw[:].bitcast(F32)
         grouped_words = grad_grouped[:].bitcast(F32)
+
+        def copy_on(engine, out, in_):
+            if engine == "scalar":
+                nc.scalar.copy(out=out, in_=in_)
+            else:
+                nc.vector.tensor_copy(out=out, in_=in_)
 
         def warm_up(count):
             for i in range(count):
@@ -76,17 +81,22 @@ def tile_transposedattentiontransformer_pb_kernel(
                     in_=w_proj[first : first + 2 * P, cols].rearrange("(p e) c -> p e c", e=2),
                 )
 
-        def load_grad(b, s, token_half):
-            tiles = slice(token_half * HALF_TILES, (token_half + 1) * HALF_TILES)
-            tokens = slice(token_half * HALF_TOKENS, (token_half + 1) * HALF_TOKENS)
+        def load_grad(b, s, first_tile, n_tiles):
+            raw = keep.tile([P, n_tiles, K_PASS], BF16, name="grad_raw_%d_%d_%d" % (b, s, first_tile))
+            tokens = slice(first_tile * P, (first_tile + n_tiles) * P)
             js = slice(s * K_PASS, (s + 1) * K_PASS)
             nc.sync.dma_start(
-                out=grad_raw[:, b, tiles, js],
-                in_=grad_out[b, tokens, js].rearrange("(i p) j -> p i j", p=P),
+                out=raw[:], in_=grad_out[b, tokens, js].rearrange("(i p) j -> p i j", p=P)
             )
+            for i in range(n_tiles):
+                grad_words[(b, s, first_tile + i)] = raw[:, i, :].bitcast(F32)
 
         def load_attn(b):
             nc.sync.dma_start(out=attn_raw[:, b, :, :], in_=attn[b].rearrange("g d e -> d g e"))
+
+        def widen_attn(engine, b, first_head, n_heads):
+            heads = slice(first_head, first_head + n_heads)
+            copy_on(engine, attn_f32[:, b, heads, :], attn_raw[:, b, heads, :])
 
         def regroup_w(pair, s):
             nc.vector.tensor_copy(
@@ -107,68 +117,79 @@ def tile_transposedattentiontransformer_pb_kernel(
             for s in range(PASSES):
                 quantise_w(pair, s)
 
-        def transpose_grad(b, s, token_half):
-            flipped = psum_in.tile([P, HALF_TILES, WORD_BLOCKS, P], F32, tag="bank")
-            for i in range(HALF_TILES):
+        def transposes(b, s, first_tile, n_tiles):
+            flipped = psum_in.tile([P, n_tiles, WORD_BLOCKS, P], F32, tag="bank")
+            for i in range(n_tiles):
                 for u in range(WORD_BLOCKS):
-                    first = (s * WORD_BLOCKS + u) * P
                     nc.tensor.transpose(
                         flipped[:, i, u, :],
-                        grad_words[:, b, token_half * HALF_TILES + i, first : first + P],
+                        grad_words[(b, s, first_tile + i)][:, u * P : (u + 1) * P],
                         identity[:],
                     )
-            if b == 0:
-                warm_up(1)
-            tokens = slice(token_half * HALF_TOKENS, (token_half + 1) * HALF_TOKENS)
-            nc.scalar.copy(
-                out=grouped_words[:, b, s, tokens, :].rearrange("p (i tok) u -> p i tok u", tok=P),
-                in_=flipped[:].rearrange("p i u tok -> p i tok u"),
+            return flipped
+
+        def gather(engine, flipped, b, s, first_tile, n_tiles):
+            tokens = slice(first_tile * P, (first_tile + n_tiles) * P)
+            copy_on(
+                engine,
+                grouped_words[:, b, s, tokens, :].rearrange("p (i tok) u -> p i tok u", tok=P),
+                flipped[:].rearrange("p i u tok -> p i tok u"),
             )
 
-        def quantise_grad(b, s, token_half):
-            tokens = slice(token_half * HALF_TOKENS, (token_half + 1) * HALF_TOKENS)
+        def transpose_grad(engine, b, s, first_tile, n_tiles):
+            gather(engine, transposes(b, s, first_tile, n_tiles), b, s, first_tile, n_tiles)
+
+        def quantise_grad(b, s, first_tile, n_tiles):
+            tokens = slice(first_tile * P, (first_tile + n_tiles) * P)
             nc.vector.quantize_mx(
                 out=grad_codes[:, b, s, tokens].bitcast(E5M2_X4),
                 scales=grad_scales[:, b, s, tokens],
                 in_=grad_grouped[:, b, s, tokens, :].rearrange("p tok t -> p (tok t)"),
             )
 
-        def prepare_grad(b, s):
-            for token_half in range(2):
-                transpose_grad(b, s, token_half)
-            for token_half in range(2):
-                quantise_grad(b, s, token_half)
-
-        def project(b, pair):
+        def open_banks():
             banks = []
             for half in range(PAIR):
                 acc = psum_in.tile([P, HEADS, HEAD_ROWS], F32, tag="bank")
                 banks.append(acc)
-            for s in range(PASSES):
-                for half in range(PAIR):
-                    cols = slice(half * HEAD_DIM, (half + 1) * HEAD_DIM)
-                    nc.tensor.matmul_mx(
-                        out=banks[half][:].rearrange("p g rr -> p (g rr)"),
-                        lhsT=w_codes[:, pair, s, cols].bitcast(E4M3_X4),
-                        lhsT_scale=w_scales[:, pair, s, cols],
-                        rhs=grad_codes[:, b, s, :].bitcast(E5M2_X4),
-                        rhs_scale=grad_scales[:, b, s, :],
-                        start=(s == 0),
-                        stop=(s == PASSES - 1),
-                    )
+            return banks
+
+        def project_pass(b, pair, s, banks):
+            for half in range(PAIR):
+                cols = slice(half * HEAD_DIM, (half + 1) * HEAD_DIM)
+                nc.tensor.matmul_mx(
+                    out=banks[half][:].rearrange("p g rr -> p (g rr)"),
+                    lhsT=w_codes[:, pair, s, cols].bitcast(E4M3_X4),
+                    lhsT_scale=w_scales[:, pair, s, cols],
+                    rhs=grad_codes[:, b, s, :].bitcast(E5M2_X4),
+                    rhs_scale=grad_scales[:, b, s, :],
+                    start=(s == 0),
+                    stop=(s == PASSES - 1),
+                )
+
+        def collect(banks, engines):
             dy_t = work.tile([P, HEADS, PAIR, HEAD_ROWS], F32, tag="dy_t")
             for group in range(HEADS // HALF_HEADS):
                 heads = slice(group * HALF_HEADS, (group + 1) * HALF_HEADS)
                 for half in range(PAIR):
-                    nc.scalar.copy(out=dy_t[:, heads, half, :], in_=banks[half][:, heads, :])
+                    copy_on(engines[half], dy_t[:, heads, half, :], banks[half][:, heads, :])
             return dy_t
 
-        def apply_attn(b, pair, dy_t):
+        def project(b, pair, engines):
+            banks = open_banks()
+            for s in range(PASSES):
+                project_pass(b, pair, s, banks)
+            return collect(banks, engines)
+
+        def apply_attn(b, pair, dy_t, groups):
             result = work.tile([P, HEADS, HEAD_DIM], F32, tag="result")
-            for group in range(HEADS // HALF_HEADS):
-                product = psum_o.tile([P, HALF_HEADS, HEAD_DIM], F32, tag="product")
-                for i in range(HALF_HEADS):
-                    g = group * HALF_HEADS + i
+            for first_head, n_heads, engine, spare_bank in groups:
+                if spare_bank:
+                    product = psum_in.tile([P, HALF_HEADS, HEAD_DIM], F32, tag="bank")
+                else:
+                    product = psum_o.tile([P, HALF_HEADS, HEAD_DIM], F32, tag="product")
+                for i in range(n_heads):
+                    g = first_head + i
                     nc.tensor.matmul(
                         out=product[:, i, :],
                         lhsT=dy_t[:, g, :, :].rearrange("p half rr -> p (half rr)"),
@@ -176,53 +197,60 @@ def tile_transposedattentiontransformer_pb_kernel(
                         start=True,
                         stop=True,
                     )
-                heads = slice(group * HALF_HEADS, (group + 1) * HALF_HEADS)
-                if group == 0:
-                    nc.scalar.copy(out=result[:, heads, :], in_=product[:])
-                else:
-                    nc.vector.tensor_copy(out=result[:, heads, :], in_=product[:])
+                heads = slice(first_head, first_head + n_heads)
+                copy_on(engine, result[:, heads, :], product[:, 0:n_heads, :])
                 for half in range(PAIR):
                     rows = slice(half * HEAD_ROWS, (half + 1) * HEAD_ROWS)
                     nc.sync.dma_start(
                         out=out_view[b, pair, half, :, heads, :], in_=result[rows, heads, :]
                     )
 
+        TWO_GROUPS = [(0, HALF_HEADS, "scalar", False), (HALF_HEADS, HALF_HEADS, "vector", False)]
+        LAST_GROUPS = [(0, 3, "scalar", False), (3, 3, "vector", False), (6, 2, "scalar", True)]
+
         for s in range(PASSES):
             load_w(0, s)
-            for token_half in range(2):
-                load_grad(0, s, token_half)
+            for h in range(2):
+                load_grad(0, s, 2 * h, 2)
         load_attn(0)
         for pair in range(1, ROUNDS):
             for s in range(PASSES):
                 load_w(pair, s)
         for s in range(PASSES):
-            for token_half in range(2):
-                load_grad(1, s, token_half)
+            for h in range(2):
+                load_grad(1, s, 2 * h, 2)
         load_attn(1)
         make_identity(nc, identity[:])
         nc.vector.memset(idle_operand[:], 0.0)
-        warm_up(6)
+        warm_up(4)
 
+        ACT2 = ("scalar", "scalar")
         for s in range(PASSES):
             regroup_w(0, s)
             quantise_w(0, s)
-            prepare_grad(0, s)
-        nc.scalar.copy(out=attn_f32[:, 0, :, :], in_=attn_raw[:, 0, :, :])
-
+            for h in range(2):
+                transpose_grad("scalar", 0, s, 2 * h, 2)
+                warm_up(1)
+            for h in range(2):
+                quantise_grad(0, s, 2 * h, 2)
+        widen_attn("scalar", 0, 0, HEADS)
         rounds = [(b, pair) for b in range(BATCH) for pair in range(ROUNDS)]
-        dy_now = project(0, 0)
+        dy_now = project(0, 0, ACT2)
         prepare_w(1)
         prepare_w(2)
-        apply_attn(0, 0, dy_now)
-        dy_now = project(0, 1)
+        apply_attn(0, 0, dy_now, TWO_GROUPS)
+        dy_now = project(0, 1, ACT2)
         for r in range(1, len(rounds)):
             if r + 2 < ROUNDS:
                 prepare_w(r + 2)
             if r == ROUNDS - 2:
                 for s in range(PASSES):
-                    prepare_grad(1, s)
-                nc.vector.tensor_copy(out=attn_f32[:, 1, :, :], in_=attn_raw[:, 1, :, :])
+                    for h in range(2):
+                        transpose_grad("scalar", 1, s, 2 * h, 2)
+                    for h in range(2):
+                        quantise_grad(1, s, 2 * h, 2)
+                widen_attn("vector", 1, 0, HEADS)
             if r + 1 < len(rounds):
-                dy_next = project(rounds[r + 1][0], rounds[r + 1][1])
-            apply_attn(rounds[r][0], rounds[r][1], dy_now)
+                dy_next = project(rounds[r + 1][0], rounds[r + 1][1], ACT2)
+            apply_attn(rounds[r][0], rounds[r][1], dy_now, TWO_GROUPS if r + 1 < len(rounds) else LAST_GROUPS)
             dy_now = dy_next

@@ -167,10 +167,10 @@ def tile_transposedattentiontransformer_pb_kernel(
                     stop=(s == PASSES - 1),
                 )
 
-        def collect(banks, engines):
+        def collect(banks, engines, head_groups):
             dy_t = work.tile([P, HEADS, PAIR, HEAD_ROWS], F32, tag="dy_t")
-            for group in range(HEADS // HALF_HEADS):
-                heads = slice(group * HALF_HEADS, (group + 1) * HALF_HEADS)
+            for first_head, n_heads in head_groups:
+                heads = slice(first_head, first_head + n_heads)
                 for half in range(PAIR):
                     copy_on(engines[half], dy_t[:, heads, half, :], banks[half][:, heads, :])
             return dy_t
@@ -179,7 +179,7 @@ def tile_transposedattentiontransformer_pb_kernel(
             banks = open_banks()
             for s in range(PASSES):
                 project_pass(b, pair, s, banks)
-            return collect(banks, engines)
+            return collect(banks, engines, FOUR_AND_FOUR)
 
         def apply_attn(b, pair, dy_t, groups):
             result = work.tile([P, HEADS, HEAD_DIM], F32, tag="result")
@@ -205,51 +205,78 @@ def tile_transposedattentiontransformer_pb_kernel(
                         out=out_view[b, pair, half, :, heads, :], in_=result[rows, heads, :]
                     )
 
+        FOUR_AND_FOUR = [(0, HALF_HEADS), (HALF_HEADS, HALF_HEADS)]
         TWO_GROUPS = [(0, HALF_HEADS, "scalar", False), (HALF_HEADS, HALF_HEADS, "vector", False)]
         LAST_GROUPS = [(0, 3, "scalar", False), (3, 3, "vector", False), (6, 2, "scalar", True)]
 
-        for s in range(PASSES):
-            load_w(0, s)
-            for h in range(2):
-                load_grad(0, s, 2 * h, 2)
+        load_w(0, 0)
+        load_grad(0, 0, 0, 2)
+        load_grad(0, 0, 2, 2)
+        load_w(0, 1)
+        load_grad(0, 1, 0, 2)
+        load_grad(0, 1, 2, 2)
+        load_grad(1, 0, 0, 2)
+        load_grad(1, 0, 2, 2)
         load_attn(0)
-        for pair in range(1, ROUNDS):
+        for s in range(PASSES):
+            load_w(1, s)
+        load_grad(1, 1, 0, 2)
+        load_grad(1, 1, 2, 2)
+        for pair in range(2, ROUNDS):
             for s in range(PASSES):
                 load_w(pair, s)
-        for s in range(PASSES):
-            for h in range(2):
-                load_grad(1, s, 2 * h, 2)
         load_attn(1)
         make_identity(nc, identity[:])
         nc.vector.memset(idle_operand[:], 0.0)
         warm_up(4)
 
         ACT2 = ("scalar", "scalar")
-        for s in range(PASSES):
-            regroup_w(0, s)
-            quantise_w(0, s)
-            for h in range(2):
-                transpose_grad("scalar", 0, s, 2 * h, 2)
-                warm_up(1)
-            for h in range(2):
-                quantise_grad(0, s, 2 * h, 2)
-        widen_attn("scalar", 0, 0, HEADS)
         rounds = [(b, pair) for b in range(BATCH) for pair in range(ROUNDS)]
-        dy_now = project(0, 0, ACT2)
+        regroup_w(0, 0)
+        quantise_w(0, 0)
+        transpose_grad("scalar", 0, 0, 0, 2)
+        warm_up(1)
+        transpose_grad("scalar", 0, 0, 2, 2)
+        warm_up(2)
+        regroup_w(0, 1)
+        quantise_grad(0, 0, 0, 2)
+        quantise_w(0, 1)
+        quantise_grad(0, 0, 2, 2)
+        transpose_grad("scalar", 0, 1, 0, 2)
+        transpose_grad("scalar", 0, 1, 2, 2)
+        warm_up(1)
+        quantise_grad(0, 1, 0, 2)
+        quantise_grad(0, 1, 2, 2)
+        widen_attn("vector", 0, 0, HALF_HEADS)
+        widen_attn("vector", 0, HALF_HEADS, HALF_HEADS)
+        banks = open_banks()
+        project_pass(0, 0, 0, banks)
+        flip_a = transposes(1, 0, 0, 2)
+        project_pass(0, 0, 1, banks)
+        flip_b = transposes(1, 0, 2, 2)
+        dy_now = collect(banks, ACT2, [(0, 2), (2, 2), (4, 4)])
+        gather("scalar", flip_a, 1, 0, 0, 2)
+        gather("scalar", flip_b, 1, 0, 2, 2)
+
         prepare_w(1)
-        prepare_w(2)
         apply_attn(0, 0, dy_now, TWO_GROUPS)
-        dy_now = project(0, 1, ACT2)
-        for r in range(1, len(rounds)):
-            if r + 2 < ROUNDS:
-                prepare_w(r + 2)
-            if r == ROUNDS - 2:
-                for s in range(PASSES):
-                    for h in range(2):
-                        transpose_grad("scalar", 1, s, 2 * h, 2)
-                    for h in range(2):
-                        quantise_grad(1, s, 2 * h, 2)
-                widen_attn("vector", 1, 0, HEADS)
+        banks = open_banks()
+        for s in range(PASSES):
+            project_pass(0, 1, s, banks)
+        flip_c = transposes(1, 1, 0, 2)
+        flip_d = transposes(1, 1, 2, 2)
+        dy_now = collect(banks, ACT2, FOUR_AND_FOUR)
+        gather("scalar", flip_c, 1, 1, 0, 2)
+        gather("scalar", flip_d, 1, 1, 2, 2)
+        prepare_w(2)
+        prepare_w(3)
+        apply_attn(0, 1, dy_now, TWO_GROUPS)
+        dy_now = project(0, 2, ACT2)
+        for s in range(PASSES):
+            for h in range(2):
+                quantise_grad(1, s, 2 * h, 2)
+        widen_attn("vector", 1, 0, HEADS)
+        for r in range(2, len(rounds)):
             if r + 1 < len(rounds):
                 dy_next = project(rounds[r + 1][0], rounds[r + 1][1], ACT2)
             apply_attn(rounds[r][0], rounds[r][1], dy_now, TWO_GROUPS if r + 1 < len(rounds) else LAST_GROUPS)

@@ -207,7 +207,7 @@ def tile_transposedattentiontransformer_pb_kernel(
 
         FOUR_AND_FOUR = [(0, HALF_HEADS), (HALF_HEADS, HALF_HEADS)]
         TWO_GROUPS = [(0, HALF_HEADS, "scalar", False), (HALF_HEADS, HALF_HEADS, "vector", False)]
-        LAST_GROUPS = [(0, 3, "scalar", False), (3, 3, "vector", False), (6, 2, "scalar", True)]
+        LAST_GROUPS = [(0, 3, "scalar", False), (3, 3, "vector", True), (6, 2, "scalar", True)]
 
         load_w(0, 0)
         load_grad(0, 0, 0, 2)

@@ -26,6 +26,9 @@ ROUNDS = FEAT // (PAIR * HEAD_DIM)
 QUARTER = PAIR * HEAD_DIM
 HALF_HEADS = HEADS // 2
 HALF_TOKENS = TOKENS // 2
+PARTS = 3
+SPLIT_HEADS = 2
+FIRST_SPLIT = HEADS - SPLIT_HEADS
 
 FLOPS = 2 * BATCH * TOKENS * FEAT * FEAT + 2 * BATCH * HEADS * TOKENS * HEAD_DIM * HEAD_DIM
 BYTES = 2 * (BATCH * TOKENS * FEAT + FEAT * FEAT + BATCH * HEADS * HEAD_DIM * HEAD_DIM) + 4 * BATCH * TOKENS * FEAT
@@ -181,7 +184,17 @@ def tile_transposedattentiontransformer_pb_kernel(
                 project_pass(b, pair, s, banks)
             return collect(banks, engines, FOUR_AND_FOUR)
 
-        def apply_attn(b, pair, dy_t, groups):
+        def split_dy(dy_t):
+            dy = dy_t[:, FIRST_SPLIT:HEADS, :, :]
+            parts = work.tile([P, PARTS, SPLIT_HEADS, PAIR, HEAD_ROWS], BF16, tag="parts")
+            rest = work.tile([P, SPLIT_HEADS, PAIR, HEAD_ROWS], F32, tag="rest")
+            nc.vector.tensor_copy(out=parts[:, 0], in_=dy)
+            nc.vector.tensor_tensor(out=rest[:], in0=dy, in1=parts[:, 0], op=mybir.AluOpType.subtract)
+            nc.vector.tensor_copy(out=parts[:, 1], in_=rest[:])
+            nc.vector.tensor_tensor(out=parts[:, 2], in0=rest[:], in1=parts[:, 1], op=mybir.AluOpType.subtract)
+            return parts
+
+        def apply_attn(b, pair, dy_t, parts, groups):
             result = work.tile([P, HEADS, HEAD_DIM], F32, tag="result")
             for first_head, n_heads, engine, spare_bank in groups:
                 if spare_bank:
@@ -190,13 +203,23 @@ def tile_transposedattentiontransformer_pb_kernel(
                     product = psum_o.tile([P, HALF_HEADS, HEAD_DIM], F32, tag="product")
                 for i in range(n_heads):
                     g = first_head + i
-                    nc.tensor.matmul(
-                        out=product[:, i, :],
-                        lhsT=dy_t[:, g, :, :].rearrange("p half rr -> p (half rr)"),
-                        rhs=attn_f32[:, b, g, :],
-                        start=True,
-                        stop=True,
-                    )
+                    if parts is not None and g >= FIRST_SPLIT:
+                        for part in range(PARTS):
+                            nc.tensor.matmul(
+                                out=product[:, i, :],
+                                lhsT=parts[:, part, g - FIRST_SPLIT, :, :].rearrange("p half rr -> p (half rr)"),
+                                rhs=attn_raw[:, b, g, :],
+                                start=(part == 0),
+                                stop=(part == PARTS - 1),
+                            )
+                    else:
+                        nc.tensor.matmul(
+                            out=product[:, i, :],
+                            lhsT=dy_t[:, g, :, :].rearrange("p half rr -> p (half rr)"),
+                            rhs=attn_f32[:, b, g, :],
+                            start=True,
+                            stop=True,
+                        )
                 heads = slice(first_head, first_head + n_heads)
                 copy_on(engine, result[:, heads, :], product[:, 0:n_heads, :])
                 for half in range(PAIR):
@@ -207,6 +230,7 @@ def tile_transposedattentiontransformer_pb_kernel(
 
         FOUR_AND_FOUR = [(0, HALF_HEADS), (HALF_HEADS, HALF_HEADS)]
         TWO_GROUPS = [(0, HALF_HEADS, "scalar", False), (HALF_HEADS, HALF_HEADS, "vector", False)]
+        BOTH_ON_SCALAR = [(0, HALF_HEADS, "scalar", False), (HALF_HEADS, HALF_HEADS, "scalar", False)]
         LAST_GROUPS = [(0, 3, "scalar", False), (3, 3, "vector", True), (6, 2, "scalar", True)]
 
         load_w(0, 0)
@@ -259,7 +283,7 @@ def tile_transposedattentiontransformer_pb_kernel(
         gather("scalar", flip_b, 1, 0, 2, 2)
 
         prepare_w(1)
-        apply_attn(0, 0, dy_now, TWO_GROUPS)
+        apply_attn(0, 0, dy_now, None, TWO_GROUPS)
         banks = open_banks()
         for s in range(PASSES):
             project_pass(0, 1, s, banks)
@@ -270,14 +294,24 @@ def tile_transposedattentiontransformer_pb_kernel(
         gather("scalar", flip_d, 1, 1, 2, 2)
         prepare_w(2)
         prepare_w(3)
-        apply_attn(0, 1, dy_now, TWO_GROUPS)
+        apply_attn(0, 1, dy_now, None, BOTH_ON_SCALAR)
         dy_now = project(0, 2, ACT2)
         for s in range(PASSES):
             for h in range(2):
                 quantise_grad(1, s, 2 * h, 2)
-        widen_attn("vector", 1, 0, HEADS)
+        parts_now = split_dy(dy_now)
         for r in range(2, len(rounds)):
             if r + 1 < len(rounds):
                 dy_next = project(rounds[r + 1][0], rounds[r + 1][1], ACT2)
-            apply_attn(rounds[r][0], rounds[r][1], dy_now, TWO_GROUPS if r + 1 < len(rounds) else LAST_GROUPS)
+                parts_next = split_dy(dy_next)
+            if r == 2:
+                groups = BOTH_ON_SCALAR
+            elif r + 1 < len(rounds):
+                groups = TWO_GROUPS
+            else:
+                groups = LAST_GROUPS
+            apply_attn(rounds[r][0], rounds[r][1], dy_now, parts_now, groups)
+            if r == 2:
+                widen_attn("vector", 1, 0, FIRST_SPLIT)
             dy_now = dy_next
+            parts_now = parts_next

@@ -27,8 +27,7 @@ QUARTER = PAIR * HEAD_DIM
 HALF_HEADS = HEADS // 2
 HALF_TOKENS = TOKENS // 2
 PARTS = 3
-SPLIT_HEADS = 2
-FIRST_SPLIT = HEADS - SPLIT_HEADS
+FIRST_SPLIT = (8, 8, 8, 5, 5, 6, 6, 6)
 
 FLOPS = 2 * BATCH * TOKENS * FEAT * FEAT + 2 * BATCH * HEADS * TOKENS * HEAD_DIM * HEAD_DIM
 BYTES = 2 * (BATCH * TOKENS * FEAT + FEAT * FEAT + BATCH * HEADS * HEAD_DIM * HEAD_DIM) + 4 * BATCH * TOKENS * FEAT
@@ -184,30 +183,34 @@ def tile_transposedattentiontransformer_pb_kernel(
                 project_pass(b, pair, s, banks)
             return collect(banks, engines, FOUR_AND_FOUR)
 
-        def split_dy(dy_t):
-            dy = dy_t[:, FIRST_SPLIT:HEADS, :, :]
-            parts = work.tile([P, PARTS, SPLIT_HEADS, PAIR, HEAD_ROWS], BF16, tag="parts")
-            rest = work.tile([P, SPLIT_HEADS, PAIR, HEAD_ROWS], F32, tag="rest")
+        def split_dy(r, dy_t):
+            n_heads = HEADS - FIRST_SPLIT[r]
+            if n_heads == 0:
+                return None
+            dy = dy_t[:, FIRST_SPLIT[r] : HEADS, :, :]
+            parts = work.tile([P, PARTS, n_heads, PAIR, HEAD_ROWS], BF16, tag="parts")
+            rest = work.tile([P, n_heads, PAIR, HEAD_ROWS], F32, tag="rest")
             nc.vector.tensor_copy(out=parts[:, 0], in_=dy)
             nc.vector.tensor_tensor(out=rest[:], in0=dy, in1=parts[:, 0], op=mybir.AluOpType.subtract)
             nc.vector.tensor_copy(out=parts[:, 1], in_=rest[:])
             nc.vector.tensor_tensor(out=parts[:, 2], in0=rest[:], in1=parts[:, 1], op=mybir.AluOpType.subtract)
             return parts
 
-        def apply_attn(b, pair, dy_t, parts, groups):
+        def apply_attn(r, dy_t, parts, groups):
+            b, pair = rounds[r]
             result = work.tile([P, HEADS, HEAD_DIM], F32, tag="result")
-            for first_head, n_heads, engine, spare_bank in groups:
+            for first_head, n_heads, engine, spare_bank, stored in groups:
                 if spare_bank:
                     product = psum_in.tile([P, HALF_HEADS, HEAD_DIM], F32, tag="bank")
                 else:
                     product = psum_o.tile([P, HALF_HEADS, HEAD_DIM], F32, tag="product")
                 for i in range(n_heads):
                     g = first_head + i
-                    if parts is not None and g >= FIRST_SPLIT:
+                    if parts is not None and g >= FIRST_SPLIT[r]:
                         for part in range(PARTS):
                             nc.tensor.matmul(
                                 out=product[:, i, :],
-                                lhsT=parts[:, part, g - FIRST_SPLIT, :, :].rearrange("p half rr -> p (half rr)"),
+                                lhsT=parts[:, part, g - FIRST_SPLIT[r], :, :].rearrange("p half rr -> p (half rr)"),
                                 rhs=attn_raw[:, b, g, :],
                                 start=(part == 0),
                                 stop=(part == PARTS - 1),
@@ -222,16 +225,18 @@ def tile_transposedattentiontransformer_pb_kernel(
                         )
                 heads = slice(first_head, first_head + n_heads)
                 copy_on(engine, result[:, heads, :], product[:, 0:n_heads, :])
-                for half in range(PAIR):
-                    rows = slice(half * HEAD_ROWS, (half + 1) * HEAD_ROWS)
-                    nc.sync.dma_start(
-                        out=out_view[b, pair, half, :, heads, :], in_=result[rows, heads, :]
-                    )
+                if stored is not None:
+                    heads = slice(stored[0], stored[0] + stored[1])
+                    for half in range(PAIR):
+                        rows = slice(half * HEAD_ROWS, (half + 1) * HEAD_ROWS)
+                        nc.sync.dma_start(
+                            out=out_view[b, pair, half, :, heads, :], in_=result[rows, heads, :]
+                        )
 
         FOUR_AND_FOUR = [(0, HALF_HEADS), (HALF_HEADS, HALF_HEADS)]
-        TWO_GROUPS = [(0, HALF_HEADS, "scalar", False), (HALF_HEADS, HALF_HEADS, "vector", False)]
-        BOTH_ON_SCALAR = [(0, HALF_HEADS, "scalar", False), (HALF_HEADS, HALF_HEADS, "scalar", False)]
-        LAST_GROUPS = [(0, 3, "scalar", False), (3, 3, "vector", True), (6, 2, "scalar", True)]
+        TWO_GROUPS = [(0, 4, "scalar", False, (0, 4)), (4, 4, "vector", False, (4, 4))]
+        BOTH_ON_SCALAR = [(0, 4, "scalar", False, (0, 4)), (4, 4, "scalar", False, (4, 4))]
+        LAST_GROUPS = [(0, 3, "scalar", True, (0, 3)), (3, 3, "vector", True, (3, 3)), (6, 2, "scalar", True, (6, 2))]
 
         load_w(0, 0)
         load_grad(0, 0, 0, 2)
@@ -266,11 +271,12 @@ def tile_transposedattentiontransformer_pb_kernel(
         quantise_grad(0, 0, 0, 2)
         quantise_w(0, 1)
         quantise_grad(0, 0, 2, 2)
-        transpose_grad("scalar", 0, 1, 0, 2)
-        transpose_grad("scalar", 0, 1, 2, 2)
+        for tile in range(TOKEN_TILES):
+            transpose_grad("scalar", 0, 1, tile, 1)
         warm_up(1)
         quantise_grad(0, 1, 0, 2)
-        quantise_grad(0, 1, 2, 2)
+        quantise_grad(0, 1, 2, 1)
+        quantise_grad(0, 1, 3, 1)
         widen_attn("vector", 0, 0, HALF_HEADS)
         widen_attn("vector", 0, HALF_HEADS, HALF_HEADS)
         banks = open_banks()
@@ -283,7 +289,7 @@ def tile_transposedattentiontransformer_pb_kernel(
         gather("scalar", flip_b, 1, 0, 2, 2)
 
         prepare_w(1)
-        apply_attn(0, 0, dy_now, None, TWO_GROUPS)
+        apply_attn(0, dy_now, None, TWO_GROUPS)
         banks = open_banks()
         for s in range(PASSES):
             project_pass(0, 1, s, banks)
@@ -294,24 +300,19 @@ def tile_transposedattentiontransformer_pb_kernel(
         gather("scalar", flip_d, 1, 1, 2, 2)
         prepare_w(2)
         prepare_w(3)
-        apply_attn(0, 1, dy_now, None, BOTH_ON_SCALAR)
+        apply_attn(1, dy_now, None, BOTH_ON_SCALAR)
         dy_now = project(0, 2, ACT2)
         for s in range(PASSES):
             for h in range(2):
                 quantise_grad(1, s, 2 * h, 2)
-        parts_now = split_dy(dy_now)
+        parts_now = split_dy(2, dy_now)
         for r in range(2, len(rounds)):
             if r + 1 < len(rounds):
                 dy_next = project(rounds[r + 1][0], rounds[r + 1][1], ACT2)
-                parts_next = split_dy(dy_next)
+                parts_next = split_dy(r + 1, dy_next)
+            groups = TWO_GROUPS if r + 1 < len(rounds) else LAST_GROUPS
+            apply_attn(r, dy_now, parts_now, groups)
             if r == 2:
-                groups = BOTH_ON_SCALAR
-            elif r + 1 < len(rounds):
-                groups = TWO_GROUPS
-            else:
-                groups = LAST_GROUPS
-            apply_attn(rounds[r][0], rounds[r][1], dy_now, parts_now, groups)
-            if r == 2:
-                widen_attn("vector", 1, 0, FIRST_SPLIT)
+                widen_attn("vector", 1, 0, 6)
             dy_now = dy_next
             parts_now = parts_next

@@ -187,13 +187,21 @@ def tile_transposedattentiontransformer_pb_kernel(
             n_heads = HEADS - FIRST_SPLIT[r]
             if n_heads == 0:
                 return None
-            dy = dy_t[:, FIRST_SPLIT[r] : HEADS, :, :]
             parts = work.tile([P, PARTS, n_heads, PAIR, HEAD_ROWS], BF16, tag="parts")
             rest = work.tile([P, n_heads, PAIR, HEAD_ROWS], F32, tag="rest")
-            nc.vector.tensor_copy(out=parts[:, 0], in_=dy)
-            nc.vector.tensor_tensor(out=rest[:], in0=dy, in1=parts[:, 0], op=mybir.AluOpType.subtract)
-            nc.vector.tensor_copy(out=parts[:, 1], in_=rest[:])
-            nc.vector.tensor_tensor(out=parts[:, 2], in0=rest[:], in1=parts[:, 1], op=mybir.AluOpType.subtract)
+            heads = range(n_heads)
+            for i in heads:
+                nc.vector.tensor_copy(out=parts[:, 0, i], in_=dy_t[:, FIRST_SPLIT[r] + i])
+            for i in heads:
+                nc.vector.tensor_tensor(
+                    out=rest[:, i], in0=dy_t[:, FIRST_SPLIT[r] + i], in1=parts[:, 0, i], op=mybir.AluOpType.subtract
+                )
+            for i in heads:
+                nc.vector.tensor_copy(out=parts[:, 1, i], in_=rest[:, i])
+            for i in heads:
+                nc.vector.tensor_tensor(
+                    out=parts[:, 2, i], in0=rest[:, i], in1=parts[:, 1, i], op=mybir.AluOpType.subtract
+                )
             return parts
 
         def apply_attn(r, dy_t, parts, groups):
@@ -271,12 +279,11 @@ def tile_transposedattentiontransformer_pb_kernel(
         quantise_grad(0, 0, 0, 2)
         quantise_w(0, 1)
         quantise_grad(0, 0, 2, 2)
-        for tile in range(TOKEN_TILES):
-            transpose_grad("scalar", 0, 1, tile, 1)
+        transpose_grad("scalar", 0, 1, 0, 2)
+        transpose_grad("scalar", 0, 1, 2, 2)
         warm_up(1)
         quantise_grad(0, 1, 0, 2)
-        quantise_grad(0, 1, 2, 1)
-        quantise_grad(0, 1, 3, 1)
+        quantise_grad(0, 1, 2, 2)
         widen_attn("vector", 0, 0, HALF_HEADS)
         widen_attn("vector", 0, HALF_HEADS, HALF_HEADS)
         banks = open_banks()

@@ -27,6 +27,7 @@ QUARTER = PAIR * HEAD_DIM
 HALF_HEADS = HEADS // 2
 HALF_TOKENS = TOKENS // 2
 PARTS = 3
+FIRST_WOVEN = (8, 8, 8, 0, 0, 0, 0, 0)
 FIRST_SPLIT = (8, 8, 8, 5, 5, 6, 6, 6)
 
 FLOPS = 2 * BATCH * TOKENS * FEAT * FEAT + 2 * BATCH * HEADS * TOKENS * HEAD_DIM * HEAD_DIM
@@ -183,28 +184,36 @@ def tile_transposedattentiontransformer_pb_kernel(
                 project_pass(b, pair, s, banks)
             return collect(banks, engines, FOUR_AND_FOUR)
 
+        def weave(r, dy_t):
+            if FIRST_WOVEN[r] == HEADS:
+                return None
+            heads = slice(FIRST_WOVEN[r], FIRST_SPLIT[r])
+            woven = work.tile([P, HEADS, HEAD_ROWS, PAIR], F32, tag="woven")
+            nc.vector.tensor_copy(
+                out=woven[:, heads, :, :], in_=dy_t[:, heads, :, :].rearrange("p g half rr -> p g rr half")
+            )
+            return woven
+
         def split_dy(r, dy_t):
             n_heads = HEADS - FIRST_SPLIT[r]
             if n_heads == 0:
                 return None
-            parts = work.tile([P, PARTS, n_heads, PAIR, HEAD_ROWS], BF16, tag="parts")
-            rest = work.tile([P, n_heads, PAIR, HEAD_ROWS], F32, tag="rest")
-            heads = range(n_heads)
-            for i in heads:
-                nc.vector.tensor_copy(out=parts[:, 0, i], in_=dy_t[:, FIRST_SPLIT[r] + i])
-            for i in heads:
-                nc.vector.tensor_tensor(
-                    out=rest[:, i], in0=dy_t[:, FIRST_SPLIT[r] + i], in1=parts[:, 0, i], op=mybir.AluOpType.subtract
-                )
-            for i in heads:
+            parts = work.tile([P, PARTS, n_heads, HEAD_ROWS, PAIR], BF16, tag="parts")
+            rest = work.tile([P, n_heads, HEAD_ROWS, PAIR], F32, tag="rest")
+            dy = [dy_t[:, FIRST_SPLIT[r] + i, :, :].rearrange("p half rr -> p rr half") for i in range(n_heads)]
+            for i in range(n_heads):
+                nc.vector.tensor_copy(out=parts[:, 0, i], in_=dy[i])
+            for i in range(n_heads):
+                nc.vector.tensor_tensor(out=rest[:, i], in0=dy[i], in1=parts[:, 0, i], op=mybir.AluOpType.subtract)
+            for i in range(n_heads):
                 nc.vector.tensor_copy(out=parts[:, 1, i], in_=rest[:, i])
-            for i in heads:
+            for i in range(n_heads):
                 nc.vector.tensor_tensor(
                     out=parts[:, 2, i], in0=rest[:, i], in1=parts[:, 1, i], op=mybir.AluOpType.subtract
                 )
             return parts
 
-        def apply_attn(r, dy_t, parts, groups):
+        def apply_attn(r, dy_t, woven, parts, groups):
             b, pair = rounds[r]
             result = work.tile([P, HEADS, HEAD_DIM], F32, tag="result")
             for first_head, n_heads, engine, spare_bank, stored in groups:
@@ -218,25 +227,28 @@ def tile_transposedattentiontransformer_pb_kernel(
                         for part in range(PARTS):
                             nc.tensor.matmul(
                                 out=product[:, i, :],
-                                lhsT=parts[:, part, g - FIRST_SPLIT[r], :, :].rearrange("p half rr -> p (half rr)"),
+                                lhsT=parts[:, part, g - FIRST_SPLIT[r], :, :].rearrange("p rr half -> p (rr half)"),
                                 rhs=attn_raw[:, b, g, :],
                                 start=(part == 0),
                                 stop=(part == PARTS - 1),
                             )
                     else:
+                        if g >= FIRST_WOVEN[r]:
+                            rows_of_head = woven[:, g, :, :].rearrange("p rr half -> p (rr half)")
+                        else:
+                            rows_of_head = dy_t[:, g, :, :].rearrange("p half rr -> p (half rr)")
                         nc.tensor.matmul(
-                            out=product[:, i, :],
-                            lhsT=dy_t[:, g, :, :].rearrange("p half rr -> p (half rr)"),
-                            rhs=attn_f32[:, b, g, :],
-                            start=True,
-                            stop=True,
+                            out=product[:, i, :], lhsT=rows_of_head, rhs=attn_f32[:, b, g, :], start=True, stop=True
                         )
                 heads = slice(first_head, first_head + n_heads)
                 copy_on(engine, result[:, heads, :], product[:, 0:n_heads, :])
                 if stored is not None:
                     heads = slice(stored[0], stored[0] + stored[1])
                     for half in range(PAIR):
-                        rows = slice(half * HEAD_ROWS, (half + 1) * HEAD_ROWS)
+                        if stored[0] >= FIRST_WOVEN[r]:
+                            rows = slice(half, P, PAIR)
+                        else:
+                            rows = slice(half * HEAD_ROWS, (half + 1) * HEAD_ROWS)
                         nc.sync.dma_start(
                             out=out_view[b, pair, half, :, heads, :], in_=result[rows, heads, :]
                         )
@@ -295,8 +307,9 @@ def tile_transposedattentiontransformer_pb_kernel(
         gather("scalar", flip_a, 1, 0, 0, 2)
         gather("scalar", flip_b, 1, 0, 2, 2)
 
+        woven_now = weave(0, dy_now)
         prepare_w(1)
-        apply_attn(0, dy_now, None, TWO_GROUPS)
+        apply_attn(0, dy_now, woven_now, None, TWO_GROUPS)
         banks = open_banks()
         for s in range(PASSES):
             project_pass(0, 1, s, banks)
@@ -305,21 +318,25 @@ def tile_transposedattentiontransformer_pb_kernel(
         dy_now = collect(banks, ACT2, FOUR_AND_FOUR)
         gather("scalar", flip_c, 1, 1, 0, 2)
         gather("scalar", flip_d, 1, 1, 2, 2)
+        woven_now = weave(1, dy_now)
         prepare_w(2)
         prepare_w(3)
-        apply_attn(1, dy_now, None, BOTH_ON_SCALAR)
+        apply_attn(1, dy_now, woven_now, None, BOTH_ON_SCALAR)
         dy_now = project(0, 2, ACT2)
         for s in range(PASSES):
             for h in range(2):
                 quantise_grad(1, s, 2 * h, 2)
+        woven_now = weave(2, dy_now)
         parts_now = split_dy(2, dy_now)
         for r in range(2, len(rounds)):
             if r + 1 < len(rounds):
                 dy_next = project(rounds[r + 1][0], rounds[r + 1][1], ACT2)
+                woven_next = weave(r + 1, dy_next)
                 parts_next = split_dy(r + 1, dy_next)
-            groups = TWO_GROUPS if r + 1 < len(rounds) else LAST_GROUPS
-            apply_attn(r, dy_now, parts_now, groups)
+            groups = BOTH_ON_SCALAR if r + 1 < len(rounds) else LAST_GROUPS
+            apply_attn(r, dy_now, woven_now, parts_now, groups)
             if r == 2:
                 widen_attn("vector", 1, 0, 6)
             dy_now = dy_next
+            woven_now = woven_next
             parts_now = parts_next

@@ -178,11 +178,11 @@ def tile_transposedattentiontransformer_pb_kernel(
                     copy_on(engines[half], dy_t[:, heads, half, :], banks[half][:, heads, :])
             return dy_t
 
-        def project(b, pair, engines):
+        def project(b, pair, engines, head_groups):
             banks = open_banks()
             for s in range(PASSES):
                 project_pass(b, pair, s, banks)
-            return collect(banks, engines, FOUR_AND_FOUR)
+            return collect(banks, engines, head_groups)
 
         def weave(r, dy_t):
             if FIRST_WOVEN[r] == HEADS:
@@ -253,6 +253,7 @@ def tile_transposedattentiontransformer_pb_kernel(
                             out=out_view[b, pair, half, :, heads, :], in_=result[rows, heads, :]
                         )
 
+        ALL_HEADS = [(0, HEADS)]
         FOUR_AND_FOUR = [(0, HALF_HEADS), (HALF_HEADS, HALF_HEADS)]
         TWO_GROUPS = [(0, 4, "scalar", False, (0, 4)), (4, 4, "vector", False, (4, 4))]
         BOTH_ON_SCALAR = [(0, 4, "scalar", False, (0, 4)), (4, 4, "scalar", False, (4, 4))]
@@ -322,15 +323,14 @@ def tile_transposedattentiontransformer_pb_kernel(
         prepare_w(2)
         prepare_w(3)
         apply_attn(1, dy_now, woven_now, None, BOTH_ON_SCALAR)
-        dy_now = project(0, 2, ACT2)
+        dy_now = project(0, 2, ACT2, FOUR_AND_FOUR)
         for s in range(PASSES):
-            for h in range(2):
-                quantise_grad(1, s, 2 * h, 2)
+            quantise_grad(1, s, 0, TOKEN_TILES)
         woven_now = weave(2, dy_now)
         parts_now = split_dy(2, dy_now)
         for r in range(2, len(rounds)):
             if r + 1 < len(rounds):
-                dy_next = project(rounds[r + 1][0], rounds[r + 1][1], ACT2)
+                dy_next = project(rounds[r + 1][0], rounds[r + 1][1], ACT2, ALL_HEADS)
                 woven_next = weave(r + 1, dy_next)
                 parts_next = split_dy(r + 1, dy_next)
             groups = BOTH_ON_SCALAR if r + 1 < len(rounds) else LAST_GROUPS

@@ -41,6 +41,7 @@ def tile_transposedattentiontransformer_pb_kernel(
     out_view = out.rearrange(
         "b g (rr pair half) e -> b pair half rr g e", pair=ROUNDS, half=PAIR
     )
+    out_rows = out.rearrange("b g (m pair) e -> b pair m g e", pair=ROUNDS)
 
     with tc.tile_pool(name="keep", bufs=1) as keep, tc.tile_pool(
         name="work", bufs=3
@@ -159,11 +160,14 @@ def tile_transposedattentiontransformer_pb_kernel(
 
         def project_pass(b, pair, s, banks):
             for half in range(PAIR):
-                cols = slice(half * HEAD_DIM, (half + 1) * HEAD_DIM)
+                chunk = PAIR * pair + half if b == 0 else pair + ROUNDS * half
+                quarter = chunk // PAIR
+                first_col = (chunk % PAIR) * HEAD_DIM
+                cols = slice(first_col, first_col + HEAD_DIM)
                 nc.tensor.matmul_mx(
                     out=banks[half][:].rearrange("p g rr -> p (g rr)"),
-                    lhsT=w_codes[:, pair, s, cols].bitcast(E4M3_X4),
-                    lhsT_scale=w_scales[:, pair, s, cols],
+                    lhsT=w_codes[:, quarter, s, cols].bitcast(E4M3_X4),
+                    lhsT_scale=w_scales[:, quarter, s, cols],
                     rhs=grad_codes[:, b, s, :].bitcast(E5M2_X4),
                     rhs_scale=grad_scales[:, b, s, :],
                     start=(s == 0),
@@ -244,20 +248,23 @@ def tile_transposedattentiontransformer_pb_kernel(
                 copy_on(engine, result[:, heads, :], product[:, 0:n_heads, :])
                 if stored is not None:
                     heads = slice(stored[0], stored[0] + stored[1])
-                    for half in range(PAIR):
-                        if stored[0] >= FIRST_WOVEN[r]:
-                            rows = slice(half, P, PAIR)
-                        else:
-                            rows = slice(half * HEAD_ROWS, (half + 1) * HEAD_ROWS)
-                        nc.sync.dma_start(
-                            out=out_view[b, pair, half, :, heads, :], in_=result[rows, heads, :]
-                        )
+                    if b == 1:
+                        nc.sync.dma_start(out=out_rows[b, pair, :, heads, :], in_=result[:, heads, :])
+                    else:
+                        for half in range(PAIR):
+                            if stored[0] >= FIRST_WOVEN[r]:
+                                rows = slice(half, P, PAIR)
+                            else:
+                                rows = slice(half * HEAD_ROWS, (half + 1) * HEAD_ROWS)
+                            nc.sync.dma_start(
+                                out=out_view[b, pair, half, :, heads, :], in_=result[rows, heads, :]
+                            )
 
         ALL_HEADS = [(0, HEADS)]
         FOUR_AND_FOUR = [(0, HALF_HEADS), (HALF_HEADS, HALF_HEADS)]
         TWO_GROUPS = [(0, 4, "scalar", False, (0, 4)), (4, 4, "vector", False, (4, 4))]
         BOTH_ON_SCALAR = [(0, 4, "scalar", False, (0, 4)), (4, 4, "scalar", False, (4, 4))]
-        LAST_GROUPS = [(0, 3, "scalar", True, (0, 3)), (3, 3, "vector", True, (3, 3)), (6, 2, "scalar", True, (6, 2))]
+        LAST_GROUPS = [(0, 3, "scalar", True, (0, 3)), (3, 2, "vector", True, (3, 2)), (5, 2, "scalar", True, (5, 2)), (7, 1, "vector", True, (7, 1))]
 
         load_w(0, 0)
         load_grad(0, 0, 0, 2)

import concourse.mybir as mybir
from concourse.masks import make_identity

BF16 = mybir.dt.bfloat16
F32 = mybir.dt.float32
U32 = mybir.dt.uint32
U8 = mybir.dt.uint8
E4M3_X4 = mybir.dt.float8_e4m3fn_x4
E5M2_X4 = mybir.dt.float8_e5m2_x4

P = 128
BATCH = 2
TOKENS = 512
FEAT = 1024
HEADS = 8
HEAD_DIM = 128
PACK = 4
K_PASS = P * PACK
PASSES = FEAT // K_PASS
WORD_BLOCKS = 2
TOKEN_TILES = TOKENS // P
HALF_TILES = TOKEN_TILES // 2
HEAD_ROWS = TOKENS // HEADS
PAIR = 2
ROUNDS = FEAT // (PAIR * HEAD_DIM)
QUARTER = PAIR * HEAD_DIM
HALF_HEADS = HEADS // 2
HALF_TOKENS = TOKENS // 2
PARTS = 3
FIRST_WOVEN = (8, 8, 8, 0, 0, 0, 0, 0)
FIRST_SPLIT = (8, 8, 8, 5, 5, 6, 6, 6)

FLOPS = 2 * BATCH * TOKENS * FEAT * FEAT + 2 * BATCH * HEADS * TOKENS * HEAD_DIM * HEAD_DIM
BYTES = 2 * (BATCH * TOKENS * FEAT + FEAT * FEAT + BATCH * HEADS * HEAD_DIM * HEAD_DIM) + 4 * BATCH * TOKENS * FEAT


def tile_transposedattentiontransformer_pb_kernel(
    tc, attn, v, w_proj, b_proj, shortcut, grad_out, out
):
    nc = tc.nc
    out_view = out.rearrange(
        "b g (rr pair half) e -> b pair half rr g e", pair=ROUNDS, half=PAIR
    )
    out_rows = out.rearrange("b g (m pair) e -> b pair m g e", pair=ROUNDS)

    with tc.tile_pool(name="keep", bufs=1) as keep, tc.tile_pool(
        name="work", bufs=3
    ) as work, tc.psum_pool(name="psum_in", bufs=6) as psum_in, tc.psum_pool(
        name="psum_o", bufs=2
    ) as psum_o, tc.manual_schedule():
        grad_words = {}
        grad_grouped = keep.tile([P, BATCH, PASSES, TOKENS, PACK], BF16, align_bytes=64)
        grad_codes = keep.tile([P, BATCH, PASSES, TOKENS], U32, align_bytes=64)
        grad_scales = keep.tile([P, BATCH, PASSES, TOKENS], U8, align_bytes=64)
        w_raw = keep.tile([P, ROUNDS, PASSES, PACK, QUARTER], BF16)
        w_grouped = keep.tile([P, ROUNDS, PASSES, QUARTER, PACK], BF16, align_bytes=64)
        w_codes = keep.tile([P, ROUNDS, PASSES, QUARTER], U32, align_bytes=64)
        w_scales = keep.tile([P, ROUNDS, PASSES, QUARTER], U8, align_bytes=64)
        attn_raw = keep.tile([P, BATCH, HEADS, HEAD_DIM], BF16)
        attn_f32 = keep.tile([P, BATCH, HEADS, HEAD_DIM], F32)
        identity = keep.tile([P, P], F32)
        idle_operand = keep.tile([P, P], F32)

        grouped_words = grad_grouped[:].bitcast(F32)

        def copy_on(engine, out, in_):
            if engine == "scalar":
                nc.scalar.copy(out=out, in_=in_)
            else:
                nc.vector.tensor_copy(out=out, in_=in_)

        def warm_up(count):
            for i in range(count):
                product = psum_o.tile([P, HALF_HEADS, HEAD_DIM], F32, tag="product")
                nc.tensor.matmul(
                    out=product[:, 0, :], lhsT=idle_operand[:], rhs=idle_operand[:], start=True, stop=True
                )

        def load_w(pair, s):
            cols = slice(pair * QUARTER, (pair + 1) * QUARTER)
            for u in range(WORD_BLOCKS):
                first = s * K_PASS + u * 2 * P
                nc.sync.dma_start(
                    out=w_raw[:, pair, s, 2 * u : 2 * u + 2, :],
                    in_=w_proj[first : first + 2 * P, cols].rearrange("(p e) c -> p e c", e=2),
                )

        def load_grad(b, s, first_tile, n_tiles):
            raw = keep.tile([P, n_tiles, K_PASS], BF16, name="grad_raw_%d_%d_%d" % (b, s, first_tile))
            tokens = slice(first_tile * P, (first_tile + n_tiles) * P)
            js = slice(s * K_PASS, (s + 1) * K_PASS)
            nc.sync.dma_start(
                out=raw[:], in_=grad_out[b, tokens, js].rearrange("(i p) j -> p i j", p=P)
            )
            for i in range(n_tiles):
                grad_words[(b, s, first_tile + i)] = raw[:, i, :].bitcast(F32)

        def load_attn(b):
            nc.sync.dma_start(out=attn_raw[:, b, :, :], in_=attn[b].rearrange("g d e -> d g e"))

        def widen_attn(engine, b, first_head, n_heads):
            heads = slice(first_head, first_head + n_heads)
            copy_on(engine, attn_f32[:, b, heads, :], attn_raw[:, b, heads, :])

        def regroup_w(pair, s):
            nc.vector.tensor_copy(
                out=w_grouped[:, pair, s, :, :].rearrange("p (c i) t -> p c t i", i=4),
                in_=w_raw[:, pair, s, :, :].rearrange("p t (c i) -> p c t i", i=4),
            )

        def quantise_w(pair, s):
            nc.vector.quantize_mx(
                out=w_codes[:, pair, s, :].bitcast(E4M3_X4),
                scales=w_scales[:, pair, s, :],
                in_=w_grouped[:, pair, s, :, :].rearrange("p c t -> p (c t)"),
            )

        def prepare_w(pair):
            for s in range(PASSES):
                regroup_w(pair, s)
            for s in range(PASSES):
                quantise_w(pair, s)

        def transposes(b, s, first_tile, n_tiles):
            flipped = psum_in.tile([P, n_tiles, WORD_BLOCKS, P], F32, tag="bank")
            for i in range(n_tiles):
                for u in range(WORD_BLOCKS):
                    nc.tensor.transpose(
                        flipped[:, i, u, :],
                        grad_words[(b, s, first_tile + i)][:, u * P : (u + 1) * P],
                        identity[:],
                    )
            return flipped

        def gather(engine, flipped, b, s, first_tile, n_tiles):
            tokens = slice(first_tile * P, (first_tile + n_tiles) * P)
            copy_on(
                engine,
                grouped_words[:, b, s, tokens, :].rearrange("p (i tok) u -> p i tok u", tok=P),
                flipped[:].rearrange("p i u tok -> p i tok u"),
            )

        def transpose_grad(engine, b, s, first_tile, n_tiles):
            gather(engine, transposes(b, s, first_tile, n_tiles), b, s, first_tile, n_tiles)

        def quantise_grad(b, s, first_tile, n_tiles):
            tokens = slice(first_tile * P, (first_tile + n_tiles) * P)
            nc.vector.quantize_mx(
                out=grad_codes[:, b, s, tokens].bitcast(E5M2_X4),
                scales=grad_scales[:, b, s, tokens],
                in_=grad_grouped[:, b, s, tokens, :].rearrange("p tok t -> p (tok t)"),
            )

        def open_banks():
            banks = []
            for half in range(PAIR):
                acc = psum_in.tile([P, HEADS, HEAD_ROWS], F32, tag="bank")
                banks.append(acc)
            return banks

        def project_pass(b, pair, s, banks):
            for half in range(PAIR):
                chunk = PAIR * pair + half if b == 0 else pair + ROUNDS * half
                quarter = chunk // PAIR
                first_col = (chunk % PAIR) * HEAD_DIM
                cols = slice(first_col, first_col + HEAD_DIM)
                nc.tensor.matmul_mx(
                    out=banks[half][:].rearrange("p g rr -> p (g rr)"),
                    lhsT=w_codes[:, quarter, s, cols].bitcast(E4M3_X4),
                    lhsT_scale=w_scales[:, quarter, s, cols],
                    rhs=grad_codes[:, b, s, :].bitcast(E5M2_X4),
                    rhs_scale=grad_scales[:, b, s, :],
                    start=(s == 0),
                    stop=(s == PASSES - 1),
                )

        def collect(banks, engines, head_groups):
            dy_t = work.tile([P, HEADS, PAIR, HEAD_ROWS], F32, tag="dy_t")
            for first_head, n_heads in head_groups:
                heads = slice(first_head, first_head + n_heads)
                for half in range(PAIR):
                    copy_on(engines[half], dy_t[:, heads, half, :], banks[half][:, heads, :])
            return dy_t

        def project(b, pair, engines, head_groups):
            banks = open_banks()
            for s in range(PASSES):
                project_pass(b, pair, s, banks)
            return collect(banks, engines, head_groups)

        def weave(r, dy_t):
            if FIRST_WOVEN[r] == HEADS:
                return None
            heads = slice(FIRST_WOVEN[r], FIRST_SPLIT[r])
            woven = work.tile([P, HEADS, HEAD_ROWS, PAIR], F32, tag="woven")
            nc.vector.tensor_copy(
                out=woven[:, heads, :, :], in_=dy_t[:, heads, :, :].rearrange("p g half rr -> p g rr half")
            )
            return woven

        def split_dy(r, dy_t):
            n_heads = HEADS - FIRST_SPLIT[r]
            if n_heads == 0:
                return None
            parts = work.tile([P, PARTS, n_heads, HEAD_ROWS, PAIR], BF16, tag="parts")
            rest = work.tile([P, n_heads, HEAD_ROWS, PAIR], F32, tag="rest")
            dy = [dy_t[:, FIRST_SPLIT[r] + i, :, :].rearrange("p half rr -> p rr half") for i in range(n_heads)]
            for i in range(n_heads):
                nc.vector.tensor_copy(out=parts[:, 0, i], in_=dy[i])
            for i in range(n_heads):
                nc.vector.tensor_tensor(out=rest[:, i], in0=dy[i], in1=parts[:, 0, i], op=mybir.AluOpType.subtract)
            for i in range(n_heads):
                nc.vector.tensor_copy(out=parts[:, 1, i], in_=rest[:, i])
            for i in range(n_heads):
                nc.vector.tensor_tensor(
                    out=parts[:, 2, i], in0=rest[:, i], in1=parts[:, 1, i], op=mybir.AluOpType.subtract
                )
            return parts

        def apply_attn(r, dy_t, woven, parts, groups):
            b, pair = rounds[r]
            result = work.tile([P, HEADS, HEAD_DIM], F32, tag="result")
            for first_head, n_heads, engine, spare_bank, stored in groups:
                if spare_bank:
                    product = psum_in.tile([P, HALF_HEADS, HEAD_DIM], F32, tag="bank")
                else:
                    product = psum_o.tile([P, HALF_HEADS, HEAD_DIM], F32, tag="product")
                for i in range(n_heads):
                    g = first_head + i
                    if parts is not None and g >= FIRST_SPLIT[r]:
                        for part in range(PARTS):
                            nc.tensor.matmul(
                                out=product[:, i, :],
                                lhsT=parts[:, part, g - FIRST_SPLIT[r], :, :].rearrange("p rr half -> p (rr half)"),
                                rhs=attn_raw[:, b, g, :],
                                start=(part == 0),
                                stop=(part == PARTS - 1),
                            )
                    else:
                        if g >= FIRST_WOVEN[r]:
                            rows_of_head = woven[:, g, :, :].rearrange("p rr half -> p (rr half)")
                        else:
                            rows_of_head = dy_t[:, g, :, :].rearrange("p half rr -> p (half rr)")
                        nc.tensor.matmul(
                            out=product[:, i, :], lhsT=rows_of_head, rhs=attn_f32[:, b, g, :], start=True, stop=True
                        )
                heads = slice(first_head, first_head + n_heads)
                copy_on(engine, result[:, heads, :], product[:, 0:n_heads, :])
                if stored is not None:
                    heads = slice(stored[0], stored[0] + stored[1])
                    if b == 1:
                        nc.sync.dma_start(out=out_rows[b, pair, :, heads, :], in_=result[:, heads, :])
                    else:
                        for half in range(PAIR):
                            if stored[0] >= FIRST_WOVEN[r]:
                                rows = slice(half, P, PAIR)
                            else:
                                rows = slice(half * HEAD_ROWS, (half + 1) * HEAD_ROWS)
                            nc.sync.dma_start(
                                out=out_view[b, pair, half, :, heads, :], in_=result[rows, heads, :]
                            )

        ALL_HEADS = [(0, HEADS)]
        FOUR_AND_FOUR = [(0, HALF_HEADS), (HALF_HEADS, HALF_HEADS)]
        TWO_GROUPS = [(0, 4, "scalar", False, (0, 4)), (4, 4, "vector", False, (4, 4))]
        BOTH_ON_SCALAR = [(0, 4, "scalar", False, (0, 4)), (4, 4, "scalar", False, (4, 4))]
        LAST_GROUPS = [(0, 3, "scalar", True, (0, 3)), (3, 2, "vector", True, (3, 2)), (5, 2, "scalar", True, (5, 2)), (7, 1, "vector", True, (7, 1))]

        load_w(0, 0)
        load_grad(0, 0, 0, 2)
        load_grad(0, 0, 2, 2)
        load_w(0, 1)
        load_grad(0, 1, 0, 2)
        load_grad(0, 1, 2, 2)
        load_grad(1, 0, 0, 2)
        load_grad(1, 0, 2, 2)
        load_attn(0)
        for s in range(PASSES):
            load_w(1, s)
        load_grad(1, 1, 0, 2)
        load_grad(1, 1, 2, 2)
        for pair in range(2, ROUNDS):
            for s in range(PASSES):
                load_w(pair, s)
        load_attn(1)
        make_identity(nc, identity[:])
        nc.vector.memset(idle_operand[:], 0.0)
        warm_up(4)

        ACT2 = ("scalar", "scalar")
        rounds = [(b, pair) for b in range(BATCH) for pair in range(ROUNDS)]
        regroup_w(0, 0)
        quantise_w(0, 0)
        transpose_grad("scalar", 0, 0, 0, 2)
        warm_up(1)
        transpose_grad("scalar", 0, 0, 2, 2)
        warm_up(2)
        regroup_w(0, 1)
        quantise_grad(0, 0, 0, 2)
        quantise_w(0, 1)
        quantise_grad(0, 0, 2, 2)
        transpose_grad("scalar", 0, 1, 0, 2)
        transpose_grad("scalar", 0, 1, 2, 2)
        warm_up(1)
        quantise_grad(0, 1, 0, 2)
        quantise_grad(0, 1, 2, 2)
        widen_attn("vector", 0, 0, HALF_HEADS)
        widen_attn("vector", 0, HALF_HEADS, HALF_HEADS)
        banks = open_banks()
        project_pass(0, 0, 0, banks)
        flip_a = transposes(1, 0, 0, 2)
        project_pass(0, 0, 1, banks)
        flip_b = transposes(1, 0, 2, 2)
        dy_now = collect(banks, ACT2, [(0, 2), (2, 2), (4, 4)])
        gather("scalar", flip_a, 1, 0, 0, 2)
        gather("scalar", flip_b, 1, 0, 2, 2)

        woven_now = weave(0, dy_now)
        prepare_w(1)
        apply_attn(0, dy_now, woven_now, None, TWO_GROUPS)
        banks = open_banks()
        for s in range(PASSES):
            project_pass(0, 1, s, banks)
        flip_c = transposes(1, 1, 0, 2)
        flip_d = transposes(1, 1, 2, 2)
        dy_now = collect(banks, ACT2, FOUR_AND_FOUR)
        gather("scalar", flip_c, 1, 1, 0, 2)
        gather("scalar", flip_d, 1, 1, 2, 2)
        woven_now = weave(1, dy_now)
        prepare_w(2)
        prepare_w(3)
        apply_attn(1, dy_now, woven_now, None, BOTH_ON_SCALAR)
        dy_now = project(0, 2, ACT2, FOUR_AND_FOUR)
        for s in range(PASSES):
            quantise_grad(1, s, 0, TOKEN_TILES)
        woven_now = weave(2, dy_now)
        parts_now = split_dy(2, dy_now)
        for r in range(2, len(rounds)):
            if r + 1 < len(rounds):
                dy_next = project(rounds[r + 1][0], rounds[r + 1][1], ACT2, ALL_HEADS)
                woven_next = weave(r + 1, dy_next)
                parts_next = split_dy(r + 1, dy_next)
            groups = BOTH_ON_SCALAR if r + 1 < len(rounds) else LAST_GROUPS
            apply_attn(r, dy_now, woven_now, parts_now, groups)
            if r == 2:
                widen_attn("vector", 1, 0, 6)
            dy_now = dy_next
            woven_now = woven_next
            parts_now = parts_next
